import numpy as np
import ml_dtypes

BF16 = ml_dtypes.bfloat16


def bf(x):
    return np.asarray(x, np.float32).astype(BF16)


def f32(x):
    return np.asarray(x, np.float32)


def f64(x):
    return np.asarray(x).astype(np.float64)


def striped(idx):
    return np.tile(idx.reshape(-1, 16).T, (8, 1))


B, HD, C, S, NP, M, N, K, H = 4, 64, 256, 1024, 128, 16, 2048, 4, 512


def setup_inputs():
    x = f32(np.random.standard_normal((C, S))).copy()
    x[:, -1] = 0.0
    idx = np.concatenate([np.random.permutation(S)[:H] for _ in range(K)])
    return {"x": x, "offs": striped(idx)}


def reference(x, offs):
    idx = offs[:16].T.reshape(-1)
    picked = f64(x)[:, idx]
    return picked.reshape(C, NP, M).max(axis=2)

@@ -1,0 +1,48 @@
+import concourse.mybir as mybir
+
+F32 = mybir.dt.float32
+U16 = mybir.dt.uint16
+
+P = 128
+CHANNELS = 256
+NODES = 1024
+LIST = 2048
+GROUP = 16
+LANES = 16
+PIECE = 512
+
+
+def tile_pooling_kernel(tc, x, offs, out):
+    nc = tc.nc
+    blocks = CHANNELS // P
+    pieces = LIST // PIECE
+    with (
+        tc.tile_pool(name="held", bufs=1) as held,
+        tc.tile_pool(name="ring", bufs=4) as ring,
+    ):
+        offsets = held.tile([P, LIST // LANES], U16, name="offsets")
+        nc.sync.dma_start(offsets[:], offs)
+
+        tables = []
+        for b in range(blocks):
+            table = held.tile([P, NODES], F32, name=f"table{b}")
+            nc.scalar.dma_start(table[:], x[b * P : (b + 1) * P, :])
+            tables.append(table)
+
+        for b in range(blocks):
+            pooled = held.tile([P, LIST // GROUP], F32, name=f"pooled{b}")
+            for k in range(pieces):
+                piece_offsets = offsets[:, k * PIECE // LANES : (k + 1) * PIECE // LANES]
+                picked = ring.tile([P, PIECE], F32, name="picked")
+                nc.scalar.activation(
+                    picked[:],
+                    tables[b][:].indirect(piece_offsets),
+                    mybir.ActivationFunctionType.Copy,
+                )
+                nc.vector.tensor_reduce(
+                    pooled[:, k * PIECE // GROUP : (k + 1) * PIECE // GROUP],
+                    picked[:].rearrange("p (n t) -> p n t", t=GROUP),
+                    axis=mybir.AxisListType.X,
+                    op=mybir.AluOpType.max,
+                )
+            nc.sync.dma_start(out[b * P : (b + 1) * P, :], pooled[:])

@@ -9,13 +9,25 @@ NODES = 1024
 LIST = 2048
 GROUP = 16
 LANES = 16
-PIECE = 512
+LARGEST = NODES
+SMALLEST = 128
+
+
+def piece_sizes(is_last_block):
+    if not is_last_block:
+        return [LARGEST] * (LIST // LARGEST)
+    sizes = []
+    left = LIST
+    while left > SMALLEST:
+        sizes.append(left // 2)
+        left -= left // 2
+    sizes.append(left)
+    return sizes
 
 
 def tile_pooling_kernel(tc, x, offs, out):
     nc = tc.nc
     blocks = CHANNELS // P
-    pieces = LIST // PIECE
     with (
         tc.tile_pool(name="held", bufs=1) as held,
         tc.tile_pool(name="ring", bufs=4) as ring,
@@ -31,18 +43,20 @@ def tile_pooling_kernel(tc, x, offs, out):
 
         for b in range(blocks):
             pooled = held.tile([P, LIST // GROUP], F32, name=f"pooled{b}")
-            for k in range(pieces):
-                piece_offsets = offsets[:, k * PIECE // LANES : (k + 1) * PIECE // LANES]
-                picked = ring.tile([P, PIECE], F32, name="picked")
+            start = 0
+            for size in piece_sizes(b == blocks - 1):
+                piece_offsets = offsets[:, start // LANES : (start + size) // LANES]
+                picked = ring.tile([P, size], F32, name="picked")
                 nc.scalar.activation(
                     picked[:],
                     tables[b][:].indirect(piece_offsets),
                     mybir.ActivationFunctionType.Copy,
                 )
                 nc.vector.tensor_reduce(
-                    pooled[:, k * PIECE // GROUP : (k + 1) * PIECE // GROUP],
+                    pooled[:, start // GROUP : (start + size) // GROUP],
                     picked[:].rearrange("p (n t) -> p n t", t=GROUP),
                     axis=mybir.AxisListType.X,
                     op=mybir.AluOpType.max,
                 )
+                start += size
             nc.sync.dma_start(out[b * P : (b + 1) * P, :], pooled[:])

@@ -9,25 +9,13 @@ NODES = 1024
 LIST = 2048
 GROUP = 16
 LANES = 16
-LARGEST = NODES
-SMALLEST = 128
-
-
-def piece_sizes(is_last_block):
-    if not is_last_block:
-        return [LARGEST] * (LIST // LARGEST)
-    sizes = []
-    left = LIST
-    while left > SMALLEST:
-        sizes.append(left // 2)
-        left -= left // 2
-    sizes.append(left)
-    return sizes
+PIECE = 1024
 
 
 def tile_pooling_kernel(tc, x, offs, out):
     nc = tc.nc
     blocks = CHANNELS // P
+    pieces = LIST // PIECE
     with (
         tc.tile_pool(name="held", bufs=1) as held,
         tc.tile_pool(name="ring", bufs=4) as ring,
@@ -43,20 +31,18 @@ def tile_pooling_kernel(tc, x, offs, out):
 
         for b in range(blocks):
             pooled = held.tile([P, LIST // GROUP], F32, name=f"pooled{b}")
-            start = 0
-            for size in piece_sizes(b == blocks - 1):
-                piece_offsets = offsets[:, start // LANES : (start + size) // LANES]
-                picked = ring.tile([P, size], F32, name="picked")
+            for k in range(pieces):
+                piece_offsets = offsets[:, k * PIECE // LANES : (k + 1) * PIECE // LANES]
+                picked = ring.tile([P, PIECE], F32, name="picked")
                 nc.scalar.activation(
                     picked[:],
                     tables[b][:].indirect(piece_offsets),
                     mybir.ActivationFunctionType.Copy,
                 )
                 nc.vector.tensor_reduce(
-                    pooled[:, start // GROUP : (start + size) // GROUP],
+                    pooled[:, k * PIECE // GROUP : (k + 1) * PIECE // GROUP],
                     picked[:].rearrange("p (n t) -> p n t", t=GROUP),
                     axis=mybir.AxisListType.X,
                     op=mybir.AluOpType.max,
                 )
-                start += size
             nc.sync.dma_start(out[b * P : (b + 1) * P, :], pooled[:])

@@ -9,40 +9,53 @@ NODES = 1024
 LIST = 2048
 GROUP = 16
 LANES = 16
-PIECE = 1024
+LARGEST = NODES
+SMALLEST = 128
+
+
+def piece_sizes(is_last_block):
+    if not is_last_block:
+        return [LARGEST] * (LIST // LARGEST)
+    sizes = []
+    left = LIST
+    while left > SMALLEST:
+        sizes.append(left // 2)
+        left -= left // 2
+    sizes.append(left)
+    return sizes
 
 
 def tile_pooling_kernel(tc, x, offs, out):
     nc = tc.nc
     blocks = CHANNELS // P
-    pieces = LIST // PIECE
     with (
         tc.tile_pool(name="held", bufs=1) as held,
         tc.tile_pool(name="ring", bufs=4) as ring,
     ):
+        tables = [held.tile([P, NODES], F32, name=f"table{b}") for b in range(blocks)]
         offsets = held.tile([P, LIST // LANES], U16, name="offsets")
-        nc.sync.dma_start(offsets[:], offs)
 
-        tables = []
-        for b in range(blocks):
-            table = held.tile([P, NODES], F32, name=f"table{b}")
-            nc.scalar.dma_start(table[:], x[b * P : (b + 1) * P, :])
-            tables.append(table)
+        nc.sync.dma_start(tables[0][:], x[0:P, :])
+        nc.sync.dma_start(offsets[:], offs)
+        for b in range(1, blocks):
+            nc.sync.dma_start(tables[b][:], x[b * P : (b + 1) * P, :])
 
         for b in range(blocks):
             pooled = held.tile([P, LIST // GROUP], F32, name=f"pooled{b}")
-            for k in range(pieces):
-                piece_offsets = offsets[:, k * PIECE // LANES : (k + 1) * PIECE // LANES]
-                picked = ring.tile([P, PIECE], F32, name="picked")
+            start = 0
+            for size in piece_sizes(b == blocks - 1):
+                piece_offsets = offsets[:, start // LANES : (start + size) // LANES]
+                picked = ring.tile([P, size], F32, name="picked")
                 nc.scalar.activation(
                     picked[:],
                     tables[b][:].indirect(piece_offsets),
                     mybir.ActivationFunctionType.Copy,
                 )
                 nc.vector.tensor_reduce(
-                    pooled[:, k * PIECE // GROUP : (k + 1) * PIECE // GROUP],
+                    pooled[:, start // GROUP : (start + size) // GROUP],
                     picked[:].rearrange("p (n t) -> p n t", t=GROUP),
                     axis=mybir.AxisListType.X,
                     op=mybir.AluOpType.max,
                 )
+                start += size
             nc.sync.dma_start(out[b * P : (b + 1) * P, :], pooled[:])

@@ -32,13 +32,19 @@ def tile_pooling_kernel(tc, x, offs, out):
         tc.tile_pool(name="held", bufs=1) as held,
         tc.tile_pool(name="ring", bufs=4) as ring,
     ):
-        tables = [held.tile([P, NODES], F32, name=f"table{b}") for b in range(blocks)]
         offsets = held.tile([P, LIST // LANES], U16, name="offsets")
-
-        nc.sync.dma_start(tables[0][:], x[0:P, :])
         nc.sync.dma_start(offsets[:], offs)
-        for b in range(1, blocks):
-            nc.sync.dma_start(tables[b][:], x[b * P : (b + 1) * P, :])
+
+        tables = []
+        for b in range(blocks):
+            table = held.tile([P, NODES], F32, name=f"table{b}")
+            nc.scalar.dma_start(table[:], x[b * P : (b + 1) * P, :])
+            tables.append(table)
+
+        cleared = held.tile([P, 1], F32, name="cleared")
+        warmed = held.tile([P, 1], F32, name="warmed")
+        nc.vector.memset(cleared[:], 0.0)
+        nc.scalar.activation(warmed[:], cleared[:], mybir.ActivationFunctionType.Copy)
 
         for b in range(blocks):
             pooled = held.tile([P, LIST // GROUP], F32, name=f"pooled{b}")

@@ -32,14 +32,13 @@ def tile_pooling_kernel(tc, x, offs, out):
         tc.tile_pool(name="held", bufs=1) as held,
         tc.tile_pool(name="ring", bufs=4) as ring,
     ):
+        tables = [held.tile([P, NODES], F32, name=f"table{b}") for b in range(blocks)]
         offsets = held.tile([P, LIST // LANES], U16, name="offsets")
-        nc.sync.dma_start(offsets[:], offs)
 
-        tables = []
-        for b in range(blocks):
-            table = held.tile([P, NODES], F32, name=f"table{b}")
-            nc.scalar.dma_start(table[:], x[b * P : (b + 1) * P, :])
-            tables.append(table)
+        nc.sync.dma_start(tables[0][:], x[0:P, :])
+        nc.sync.dma_start(offsets[:], offs)
+        for b in range(1, blocks):
+            nc.sync.dma_start(tables[b][:], x[b * P : (b + 1) * P, :])
 
         cleared = held.tile([P, 1], F32, name="cleared")
         warmed = held.tile([P, 1], F32, name="warmed")

@@ -10,6 +10,7 @@ LIST = 2048
 GROUP = 16
 LANES = 16
 LARGEST = NODES
+HALVES = 2
 SMALLEST = 128
 
 
@@ -35,7 +36,9 @@ def tile_pooling_kernel(tc, x, offs, out):
         tables = [held.tile([P, NODES], F32, name=f"table{b}") for b in range(blocks)]
         offsets = held.tile([P, LIST // LANES], U16, name="offsets")
 
-        nc.sync.dma_start(tables[0][:], x[0:P, :])
+        for h in range(HALVES):
+            columns = slice(h * NODES // HALVES, (h + 1) * NODES // HALVES)
+            nc.sync.dma_start(tables[0][:, columns], x[0:P, columns])
         nc.sync.dma_start(offsets[:], offs)
         for b in range(1, blocks):
             nc.sync.dma_start(tables[b][:], x[b * P : (b + 1) * P, :])

@@ -50,8 +50,10 @@ def tile_pooling_kernel(tc, x, offs, out):
 
         for b in range(blocks):
             pooled = held.tile([P, LIST // GROUP], F32, name=f"pooled{b}")
+            sizes = piece_sizes(b == blocks - 1)
+            early = (LIST - sizes[-1]) // GROUP
             start = 0
-            for size in piece_sizes(b == blocks - 1):
+            for size in sizes:
                 piece_offsets = offsets[:, start // LANES : (start + size) // LANES]
                 picked = ring.tile([P, size], F32, name="picked")
                 nc.scalar.activation(
@@ -66,4 +68,6 @@ def tile_pooling_kernel(tc, x, offs, out):
                     op=mybir.AluOpType.max,
                 )
                 start += size
-            nc.sync.dma_start(out[b * P : (b + 1) * P, :], pooled[:])
+                if start // GROUP == early:
+                    nc.sync.dma_start(out[b * P : (b + 1) * P, :early], pooled[:, :early])
+            nc.sync.dma_start(out[b * P : (b + 1) * P, early:], pooled[:, early:])

@@ -51,7 +51,7 @@ def tile_pooling_kernel(tc, x, offs, out):
         for b in range(blocks):
             pooled = held.tile([P, LIST // GROUP], F32, name=f"pooled{b}")
             sizes = piece_sizes(b == blocks - 1)
-            early = (LIST - sizes[-1]) // GROUP
+            early = (LIST - sizes[-1]) // GROUP if b == blocks - 1 else LIST // GROUP
             start = 0
             for size in sizes:
                 piece_offsets = offsets[:, start // LANES : (start + size) // LANES]
@@ -70,4 +70,4 @@ def tile_pooling_kernel(tc, x, offs, out):
                 start += size
                 if start // GROUP == early:
                     nc.sync.dma_start(out[b * P : (b + 1) * P, :early], pooled[:, :early])
-            nc.sync.dma_start(out[b * P : (b + 1) * P, early:], pooled[:, early:])
+        nc.sync.dma_start(out[b * P : (b + 1) * P, early:], pooled[:, early:])

@@ -10,7 +10,6 @@ LIST = 2048
 GROUP = 16
 LANES = 16
 LARGEST = NODES
-HALVES = 2
 SMALLEST = 128
 
 
@@ -36,9 +35,7 @@ def tile_pooling_kernel(tc, x, offs, out):
         tables = [held.tile([P, NODES], F32, name=f"table{b}") for b in range(blocks)]
         offsets = held.tile([P, LIST // LANES], U16, name="offsets")
 
-        for h in range(HALVES):
-            columns = slice(h * NODES // HALVES, (h + 1) * NODES // HALVES)
-            nc.sync.dma_start(tables[0][:, columns], x[0:P, columns])
+        nc.sync.dma_start(tables[0][:], x[0:P, :])
         nc.sync.dma_start(offsets[:], offs)
         for b in range(1, blocks):
             nc.sync.dma_start(tables[b][:], x[b * P : (b + 1) * P, :])

@@ -32,13 +32,17 @@ def tile_pooling_kernel(tc, x, offs, out):
         tc.tile_pool(name="held", bufs=1) as held,
         tc.tile_pool(name="ring", bufs=4) as ring,
     ):
+        x_rows = x.rearrange("(p b) n -> b p n", b=blocks)
+        out_rows = out.rearrange("(p b) i -> b p i", b=blocks)
+        x_blocks = [x_rows[b] for b in range(blocks)]
+        out_blocks = [out_rows[b] for b in range(blocks)]
         tables = [held.tile([P, NODES], F32, name=f"table{b}") for b in range(blocks)]
         offsets = held.tile([P, LIST // LANES], U16, name="offsets")
 
-        nc.sync.dma_start(tables[0][:], x[0:P, :])
+        nc.sync.dma_start(tables[0][:], x_blocks[0])
         nc.sync.dma_start(offsets[:], offs)
         for b in range(1, blocks):
-            nc.sync.dma_start(tables[b][:], x[b * P : (b + 1) * P, :])
+            nc.sync.dma_start(tables[b][:], x_blocks[b])
 
         cleared = held.tile([P, 1], F32, name="cleared")
         warmed = held.tile([P, 1], F32, name="warmed")
@@ -66,5 +70,5 @@ def tile_pooling_kernel(tc, x, offs, out):
                 )
                 start += size
                 if start // GROUP == early:
-                    nc.sync.dma_start(out[b * P : (b + 1) * P, :early], pooled[:, :early])
-        nc.sync.dma_start(out[b * P : (b + 1) * P, early:], pooled[:, early:])
+                    nc.sync.dma_start(out_blocks[b][:, :early], pooled[:, :early])
+        nc.sync.dma_start(out_blocks[b][:, early:], pooled[:, early:])

@@ -10,19 +10,13 @@ LIST = 2048
 GROUP = 16
 LANES = 16
 LARGEST = NODES
-SMALLEST = 128
 
 
 def piece_sizes(is_last_block):
     if not is_last_block:
         return [LARGEST] * (LIST // LARGEST)
-    sizes = []
-    left = LIST
-    while left > SMALLEST:
-        sizes.append(left // 2)
-        left -= left // 2
-    sizes.append(left)
-    return sizes
+    quarter = LIST // 4
+    return [LIST // 2, quarter, quarter * 5 // 8, quarter * 3 // 8]
 
 
 def tile_pooling_kernel(tc, x, offs, out):
@@ -52,7 +46,7 @@ def tile_pooling_kernel(tc, x, offs, out):
         for b in range(blocks):
             pooled = held.tile([P, LIST // GROUP], F32, name=f"pooled{b}")
             sizes = piece_sizes(b == blocks - 1)
-            early = (LIST - sizes[-1]) // GROUP if b == blocks - 1 else LIST // GROUP
+            early = sum(sizes[:-2]) // GROUP if b == blocks - 1 else LIST // GROUP
             start = 0
             for size in sizes:
                 piece_offsets = offsets[:, start // LANES : (start + size) // LANES]

import concourse.mybir as mybir

F32 = mybir.dt.float32
U16 = mybir.dt.uint16

P = 128
CHANNELS = 256
NODES = 1024
LIST = 2048
GROUP = 16
LANES = 16
LARGEST = NODES


def piece_sizes(is_last_block):
    if not is_last_block:
        return [LARGEST] * (LIST // LARGEST)
    quarter = LIST // 4
    return [LIST // 2, quarter, quarter * 5 // 8, quarter * 3 // 8]


def tile_pooling_kernel(tc, x, offs, out):
    nc = tc.nc
    blocks = CHANNELS // P
    with (
        tc.tile_pool(name="held", bufs=1) as held,
        tc.tile_pool(name="ring", bufs=4) as ring,
    ):
        x_rows = x.rearrange("(p b) n -> b p n", b=blocks)
        out_rows = out.rearrange("(p b) i -> b p i", b=blocks)
        x_blocks = [x_rows[b] for b in range(blocks)]
        out_blocks = [out_rows[b] for b in range(blocks)]
        tables = [held.tile([P, NODES], F32, name=f"table{b}") for b in range(blocks)]
        offsets = held.tile([P, LIST // LANES], U16, name="offsets")

        nc.sync.dma_start(tables[0][:], x_blocks[0])
        nc.sync.dma_start(offsets[:], offs)
        for b in range(1, blocks):
            nc.sync.dma_start(tables[b][:], x_blocks[b])

        cleared = held.tile([P, 1], F32, name="cleared")
        warmed = held.tile([P, 1], F32, name="warmed")
        nc.vector.memset(cleared[:], 0.0)
        nc.scalar.activation(warmed[:], cleared[:], mybir.ActivationFunctionType.Copy)

        for b in range(blocks):
            pooled = held.tile([P, LIST // GROUP], F32, name=f"pooled{b}")
            sizes = piece_sizes(b == blocks - 1)
            early = sum(sizes[:-2]) // GROUP if b == blocks - 1 else LIST // GROUP
            start = 0
            for size in sizes:
                piece_offsets = offsets[:, start // LANES : (start + size) // LANES]
                picked = ring.tile([P, size], F32, name="picked")
                nc.scalar.activation(
                    picked[:],
                    tables[b][:].indirect(piece_offsets),
                    mybir.ActivationFunctionType.Copy,
                )
                nc.vector.tensor_reduce(
                    pooled[:, start // GROUP : (start + size) // GROUP],
                    picked[:].rearrange("p (n t) -> p n t", t=GROUP),
                    axis=mybir.AxisListType.X,
                    op=mybir.AluOpType.max,
                )
                start += size
                if start // GROUP == early:
                    nc.sync.dma_start(out_blocks[b][:, :early], pooled[:, :early])
        nc.sync.dma_start(out_blocks[b][:, early:], pooled[:, early:])
